import numpy as np
import ml_dtypes


def mxq(x, axis, fmt="e4m3"):
    dtype, down = {"e4m3": (ml_dtypes.float8_e4m3fn, 7), "e5m2": (ml_dtypes.float8_e5m2, 14)}[fmt]
    v = np.moveaxis(np.asarray(x, np.float32).astype(ml_dtypes.bfloat16).astype(np.float64), axis, -1)
    blocks = v.reshape(v.shape[:-1] + (-1, 32))
    amax = np.abs(blocks).max(-1, keepdims=True)
    byte = np.maximum(np.where(amax > 0, np.frexp(amax)[1] - 1 + 127, 0) - down, 1)
    scale = np.exp2(byte - 127.0)
    codes = (blocks / scale).astype(np.float32).astype(dtype).astype(np.float64)
    return np.moveaxis((codes * scale).reshape(v.shape), -1, axis)


WIDE = False


def mx_kscale(k):
    if not WIDE:
        return np.ones(k)
    levels = np.array([10, -10, 5, -5, 0])
    if k % 512:
        return np.exp2(np.random.permutation(np.resize(levels, k // 32))).repeat(32)
    a = np.empty((k // 512, 16))
    for p in range(k // 512):
        a[p, :8] = np.random.permutation(np.resize(levels, 8))
        for g in range(8):
            far = levels[np.abs(levels - a[p, g]) >= 10]
            a[p, g + 8] = far[np.random.randint(len(far))]
    return np.exp2(a.ravel()).repeat(32)


BF16 = ml_dtypes.bfloat16


def bf(x):
    return np.asarray(x, np.float32).astype(BF16)


def f64(x):
    return np.asarray(x).astype(np.float64)


E, F, H, MID, OUT = 4096, 64, 192, 1024, 256
D = 2 * (F + H)
IN = D + 1


def draw0():
    s = mx_kscale(D)
    t = mx_kscale(MID)
    w1 = np.concatenate([np.random.standard_normal((MID, D)) / np.sqrt(D) / s[None, :],
                         np.random.standard_normal((MID, 1)) * 0.5], axis=1) * t[:, None]
    return {"dst_node_feat": bf(np.random.standard_normal((E, F)) * s[:F]),
            "dst_node_hidden": bf(np.random.standard_normal((E, H)) * s[F:F + H]),
            "src_node_feat": bf(np.random.standard_normal((E, F)) * s[F + H:2 * F + H]),
            "src_node_hidden": bf(np.random.standard_normal((E, H)) * s[2 * F + H:]),
            "edge_feat": bf(np.random.standard_normal(E)),
            "W1": bf(w1),
            "b1": bf(np.random.standard_normal(MID) * 0.3 * t),
            "W2": bf(np.random.standard_normal((OUT, MID)) / np.sqrt(MID) / t[None, :]),
            "b2": bf(np.random.standard_normal(OUT) * 0.3)}


def core(dst_node_feat, dst_node_hidden, src_node_feat, src_node_hidden, edge_feat, W1, b1, W2, b2):
    x = np.concatenate([f64(dst_node_feat), f64(dst_node_hidden), f64(src_node_feat), f64(src_node_hidden),
                        f64(edge_feat)[:, None]], axis=1)
    w1 = f64(W1)
    pre = (mxq(x[:, :D], 1, "e4m3") @ mxq(w1[:, :D], 1, "e4m3").T) + x[:, D:] * w1[:, D] + f64(b1)
    h = np.maximum(pre, 0.0)
    return np.tanh((mxq(h, 1, "e4m3") @ mxq(f64(W2), 1, "e4m3").T) + f64(b2))


def e4m3fn_bytes(y):
    return np.clip(np.asarray(y, np.float64), -448.0, 448.0).astype(np.float32).astype(ml_dtypes.float8_e4m3fn).view(np.uint8)


def e4m3fn_values(b):
    return np.asarray(b, np.uint8).view(ml_dtypes.float8_e4m3fn).astype(np.float64)


def setup_inputs():
    d = draw0()
    x0 = np.asarray(d['src_node_hidden']).astype(np.float64)
    s = (np.max(np.abs(x0), axis=(0,), keepdims=True) / 448.0).astype(np.float32)
    out = {}
    for k, v in d.items():
        if k == 'src_node_hidden':
            out['src_node_hidden_bytes'] = e4m3fn_bytes(x0 / s.astype(np.float64))
            out['src_node_hidden_scale'] = s
        else:
            out[k] = v
    return out


def reference(dst_node_feat, dst_node_hidden, src_node_feat, src_node_hidden_bytes, src_node_hidden_scale, edge_feat, W1, b1, W2, b2):
    return core(dst_node_feat, dst_node_hidden, src_node_feat, e4m3fn_values(src_node_hidden_bytes) * src_node_hidden_scale.astype(np.float64), edge_feat, W1, b1, W2, b2)

@@ -1,0 +1,368 @@
+from contextlib import ExitStack
+
+import concourse.mybir as mybir
+from concourse.masks import make_identity
+
+F32 = mybir.dt.float32
+BF16 = mybir.dt.bfloat16
+U32 = mybir.dt.uint32
+U8 = mybir.dt.uint8
+FP8 = mybir.dt.float8_e4m3fn
+FP8X4 = mybir.dt.float8_e4m3fn_x4
+ADD = mybir.AluOpType.add
+MULT = mybir.AluOpType.mult
+MAX = mybir.AluOpType.max
+ACT = mybir.ActivationFunctionType
+
+P = 128
+E, F, H, MID, OUT = 4096, 64, 192, 1024, 256
+D = 2 * (F + H)
+FLOPS = 2 * E * (D + 1) * MID + 2 * E * MID * OUT
+
+TOK = 512
+TILES = E // TOK
+SUBS = TOK // P
+ROW = 544
+
+
+def tile_edgenetwork_t_kernel(tc, dst_feat, dst_hidden, src_feat, src_bytes, src_scale,
+                                          edge, w1, b1, w2, b2, out):
+    nc = tc.nc
+    with ExitStack() as ctx:
+        keep = ctx.enter_context(tc.tile_pool(name="keep", bufs=1))
+        work = ctx.enter_context(tc.tile_pool(name="work", bufs=2))
+        psum = ctx.enter_context(tc.psum_pool(name="psum", bufs=2))
+        ctx.enter_context(tc.manual_schedule())
+
+        ident = keep.tile([P, P], F32, name="ident")
+        make_identity(nc, ident[:])
+        warm = keep.tile([P, 1], F32, name="warm")
+        nc.vector.memset(warm[:], 0.0)
+        nc.scalar.activation(out=warm[:], in_=warm[:], func=ACT.Tanh)
+
+        scale_bc = keep.tile([P, H], F32, name="scale_bc")
+        edge_bc = [keep.tile([P, TOK], BF16, name=f"edge_bc{i}") for i in range(TILES)]
+        x_rows = [keep.tile([P, SUBS, D], BF16, name=f"x_rows{i}", align_bytes=64) for i in range(TILES)]
+        x_bytes = [keep.tile([P, SUBS, H], U8, name=f"x_bytes{i}", align_bytes=64) for i in range(TILES)]
+        w1_rows = [keep.tile([P, 4, ROW], BF16, name=f"w1_rows{h}", align_bytes=64) for h in range(2)]
+        w2_rows = keep.tile([P, 2, MID], BF16, name="w2_rows", align_bytes=64)
+        b1_bf = keep.tile([P, 2, 4], BF16, name="b1_bf")
+        b2_bf = keep.tile([P, 2], BF16, name="b2_bf")
+
+        def rows(ap, i):
+            return ap[TOK * i:TOK * (i + 1), :].rearrange("(s p) f -> p s f", p=P)
+
+        def load_x(i):
+            nc.sync.dma_start(out=x_bytes[i][:], in_=rows(src_bytes, i))
+            nc.sync.dma_start(out=x_rows[i][:, :, 0:F], in_=rows(dst_feat, i))
+            nc.sync.dma_start(out=x_rows[i][:, :, F:F + H], in_=rows(dst_hidden, i))
+            nc.sync.dma_start(out=x_rows[i][:, :, F + H:2 * F + H], in_=rows(src_feat, i))
+
+        def load_edge(i):
+            nc.sync.dma_start(out=edge_bc[i][:], in_=edge[TOK * i:TOK * (i + 1)].partition_broadcast(P))
+
+        def load_w1(h):
+            nc.sync.dma_start(out=w1_rows[h][:, :, 0:D + 1],
+                              in_=w1[512 * h:512 * (h + 1), :].rearrange("(p t) k -> p t k", t=4))
+
+        nc.sync.dma_start(out=scale_bc[:], in_=src_scale.rearrange("o k -> (o k)").partition_broadcast(P))
+        load_x(0)
+        load_w1(0)
+        nc.sync.dma_start(out=b1_bf[:], in_=b1.rearrange("(h p t) -> p h t", h=2, t=4))
+        load_edge(0)
+        load_w1(1)
+        load_x(1)
+        load_edge(1)
+        nc.sync.dma_start(out=w2_rows[:], in_=w2.rearrange("(p c) k -> p c k", c=2))
+        nc.sync.dma_start(out=b2_bf[:], in_=b2.rearrange("(p c) -> p c", c=2))
+        for i in range(2, TILES):
+            load_x(i)
+            load_edge(i)
+
+        w_col = keep.tile([P, 2, 4], F32, name="w_col")
+        b1_col = keep.tile([P, 2, 4], F32, name="b1_col")
+        b2_col = keep.tile([P, 2], F32, name="b2_col")
+        w1_words = [keep.tile([P, 512, 2], F32, name=f"w1_words{h}", align_bytes=64) for h in range(2)]
+        w2_words = keep.tile([P, 512, 2], F32, name="w2_words", align_bytes=64)
+        w1_codes = [keep.tile([P, 512], U32, name=f"w1_codes{h}", align_bytes=64) for h in range(2)]
+        w1_scales = [keep.tile([P, 512], U8, name=f"w1_scales{h}", align_bytes=64) for h in range(2)]
+        w2_codes = keep.tile([P, 512], U32, name="w2_codes", align_bytes=64)
+        w2_scales = keep.tile([P, 512], U8, name="w2_scales", align_bytes=64)
+
+        def quantize(codes, scales, words):
+            nc.vector.quantize_mx(out=codes[:].bitcast(FP8X4), scales=scales[:],
+                                  in_=words[:].rearrange("p n u -> p (n u)").bitcast(BF16))
+
+        def bank4():
+            return psum.tile([P, 2, 2, P], F32, name="turned", bufs=2)
+
+        def turn(bank, pairs):
+            for a, words in enumerate(pairs):
+                for u in range(2):
+                    nc.tensor.transpose(bank[:, a, u, :], words[:, u:256:2], ident[:])
+
+        def copy(eng, out_ap, in_ap):
+            if eng == "s":
+                nc.scalar.copy(out=out_ap, in_=in_ap)
+            else:
+                nc.vector.tensor_copy(out=out_ap, in_=in_ap)
+
+        def unbank(eng, words, half, bank):
+            copy(eng, words[:, 256 * half:256 * (half + 1), :].rearrange("p (a n) u -> p a n u", a=2),
+                 bank[:].rearrange("p a u n -> p a n u"))
+
+        xw, xc, xs, banks = {}, {}, {}, {}
+
+        def widen(i, s):
+            nc.vector.tensor_tensor(out=x_rows[i][:, s, 2 * F + H:D], in0=x_bytes[i][:, s, :].bitcast(FP8),
+                                    in1=scale_bc[:], op=MULT)
+
+        def turn_x(i, half):
+            bank = bank4()
+            banks[i, half] = bank
+            turn(bank, [x_rows[i][:, 2 * half + a, :].bitcast(F32) for a in range(2)])
+
+        def copy_x(eng, i, half):
+            if half == 0:
+                xt = work.tile([P, TOK, 2], F32, name="x_words", align_bytes=64)
+                xw[i] = xt
+            unbank(eng, xw[i], half, banks.pop((i, half)))
+
+        def quant_x(i):
+            codes = work.tile([P, TOK], U32, name="x_codes", align_bytes=64)
+            scales = work.tile([P, TOK], U8, name="x_scales", align_bytes=64)
+            quantize(codes, scales, xw[i])
+            xc[i], xs[i] = codes, scales
+
+        cs = {}
+
+        def make_c(eng, i, ht):
+            if i not in cs:
+                ct = work.tile([P, 8, TOK], F32, name="edge_term")
+                cs[i] = ct
+            h, t = ht // 4, ht % 4
+            o, w_ap, b_ap = cs[i][:, ht, :], w_col[:, h, t:t + 1], b1_col[:, h, t:t + 1]
+            if eng == "s":
+                nc.scalar.activation(out=o, in_=edge_bc[i][:], func=ACT.Identity, scale=w_ap, bias=b_ap)
+            elif eng == "v":
+                nc.vector.tensor_scalar(out=o, in0=edge_bc[i][:], scalar1=w_ap, scalar2=b_ap, op0=MULT, op1=ADD)
+            else:
+                nc.gpsimd.tensor_scalar(out=o, in0=edge_bc[i][:], scalar1=w_ap, scalar2=b_ap, op0=MULT, op1=ADD)
+
+        mm, hb, hc, hs = {}, {}, {}, {}
+
+        def layer1(i, j):
+            h, s = j // 4, j % 4
+            acc = psum.tile([P, 4, P], F32, name="acc", bufs=4)
+            for t in range(4):
+                nc.tensor.matmul_mx(out=acc[:, t, :],
+                                    lhsT=w1_codes[h][:, P * t:P * (t + 1)].bitcast(FP8X4),
+                                    lhsT_scale=w1_scales[h][:, P * t:P * (t + 1)],
+                                    rhs=xc[i][:, P * s:P * (s + 1)].bitcast(FP8X4),
+                                    rhs_scale=xs[i][:, P * s:P * (s + 1)], start=True, stop=True)
+            mm[i, j] = acc
+
+        def add(i, j):
+            h, s = j // 4, j % 4
+            if s == 0:
+                ht = work.tile([P, TOK, 4], BF16, name="hidden", bufs=3, align_bytes=64)
+                hb[i, h] = ht
+            nc.vector.tensor_tensor(out=hb[i, h][:, P * s:P * (s + 1), :],
+                                    in0=mm.pop((i, j))[:].rearrange("p t n -> p n t"),
+                                    in1=cs[i][:, 4 * h:4 * (h + 1), P * s:P * (s + 1)].rearrange("p t n -> p n t"),
+                                    op=ADD)
+
+        def relu(eng, i, h, lo=0, hi=TOK):
+            part = hb[i, h][:, lo:hi, :]
+            if eng == "s":
+                nc.scalar.activation(out=part, in_=part, func=ACT.Relu)
+            else:
+                nc.vector.tensor_scalar_max(out=part, in0=part, scalar1=0.0)
+
+        def quant_h(i, h, lo=0, hi=TOK):
+            if lo == 0:
+                codes = work.tile([P, TOK], U32, name="h_codes", bufs=4, align_bytes=64)
+                scales = work.tile([P, TOK], U8, name="h_scales", bufs=4, align_bytes=64)
+                hc[i, h], hs[i, h] = codes, scales
+            nc.vector.quantize_mx(out=hc[i, h][:, lo:hi].bitcast(FP8X4), scales=hs[i, h][:, lo:hi],
+                                  in_=hb[i, h][:, lo:hi, :].rearrange("p n t -> p (n t)"))
+
+        l2, ob = {}, {}
+
+        def layer2(i):
+            for c in range(2):
+                acc2 = psum.tile([P, TOK], F32, name="acc2", bufs=2)
+                for h in range(2):
+                    w0 = 256 * h + P * c
+                    nc.tensor.matmul_mx(out=acc2[:],
+                                        lhsT=w2_codes[:, w0:w0 + P].bitcast(FP8X4), lhsT_scale=w2_scales[:, w0:w0 + P],
+                                        rhs=hc[i, h][:].bitcast(FP8X4), rhs_scale=hs[i, h][:],
+                                        start=(h == 0), stop=(h == 1))
+                l2[i, c] = acc2
+
+        def layer2_half(i, half):
+            n0 = 256 * half
+            acc2 = psum.tile([P, 2, 256], F32, name="acc2", bufs=2)
+            for c in range(2):
+                for h in range(2):
+                    w0 = 256 * h + P * c
+                    nc.tensor.matmul_mx(out=acc2[:, c, :],
+                                        lhsT=w2_codes[:, w0:w0 + P].bitcast(FP8X4), lhsT_scale=w2_scales[:, w0:w0 + P],
+                                        rhs=hc[i, h][:, n0:n0 + 256].bitcast(FP8X4), rhs_scale=hs[i, h][:, n0:n0 + 256],
+                                        start=(h == 0), stop=(h == 1))
+            if half == 0:
+                ot = work.tile([P, 2, TOK], F32, name="channels")
+                ob[i] = ot
+            l2[i, half] = acc2
+
+        def tanh_half(i, half):
+            acc2 = l2.pop((i, half))
+            for c in range(2):
+                nc.scalar.activation(out=ob[i][:, c, 256 * half:256 * (half + 1)], in_=acc2[:, c, :],
+                                     func=ACT.Tanh, bias=b2_col[:, c:c + 1])
+
+        def tanh(i, c):
+            if c == 0:
+                ot = work.tile([P, 2, TOK], F32, name="channels")
+                ob[i] = ot
+            nc.scalar.activation(out=ob[i][:, c, :], in_=l2.pop((i, c))[:], func=ACT.Tanh, bias=b2_col[:, c:c + 1])
+
+        def turn_out(i, half):
+            bank = bank4()
+            banks["o", i, half] = bank
+            for a in range(2):
+                s = 2 * half + a
+                for c in range(2):
+                    nc.tensor.transpose(bank[:, a, c, :], ob[i][:, c, P * s:P * (s + 1)], ident[:])
+
+        def store(eng, i, half):
+            res = work.tile([P, 2, OUT], F32, name="result", bufs=4)
+            copy(eng, res[:].rearrange("p a (q c) -> p a q c", c=2),
+                 banks.pop(("o", i, half))[:].rearrange("p a c q -> p a q c"))
+            r0 = TOK * i + 2 * P * half
+            nc.sync.dma_start(out=out[r0:r0 + 2 * P, :].rearrange("(a p) f -> p a f", p=P), in_=res[:])
+
+        def turn_w1(h, half):
+            bank = bank4()
+            banks["w", h, half] = bank
+            turn(bank, [w1_rows[h][:, 2 * half + a, 0:D].bitcast(F32) for a in range(2)])
+
+        def turn_w2(h):
+            bank = bank4()
+            banks["w2", h] = bank
+            turn(bank, [w2_rows[:, c, 512 * h:512 * (h + 1)].bitcast(F32) for c in range(2)])
+
+        nc.gpsimd.tensor_copy(out=b1_col[:], in_=b1_bf[:])
+        nc.gpsimd.tensor_copy(out=w_col[:, 0, :], in_=w1_rows[0][:, :, D])
+        nc.gpsimd.tensor_copy(out=w_col[:, 1, :], in_=w1_rows[1][:, :, D])
+        nc.gpsimd.tensor_copy(out=b2_col[:], in_=b2_bf[:])
+
+        for s in range(4):
+            widen(0, s)
+        turn_x(0, 0)
+        turn_x(0, 1)
+        copy_x("v", 0, 0)
+        copy_x("s", 0, 1)
+        turn_w1(0, 0)
+        turn_w1(0, 1)
+        quant_x(0)
+        unbank("s", w1_words[0], 0, banks.pop(("w", 0, 0)))
+        unbank("v", w1_words[0], 1, banks.pop(("w", 0, 1)))
+        make_c("s", 0, 0)
+        make_c("v", 0, 2)
+        quantize(w1_codes[0], w1_scales[0], w1_words[0])
+        make_c("v", 0, 3)
+        make_c("s", 0, 1)
+        turn_w1(1, 0)
+        turn_w1(1, 1)
+        unbank("s", w1_words[1], 0, banks.pop(("w", 1, 0)))
+
+        last = TILES - 1
+        for i in range(TILES):
+            nxt = i < last
+            prev = i > 0
+            for j in range(8):
+                layer1(i, j)
+                add(i, j)
+                if i == 0:
+                    if j == 0:
+                        unbank("v", w1_words[1], 1, banks.pop(("w", 1, 1)))
+                        for t in range(4, 8):
+                            make_c("s", 0, t)
+                        widen(1, 0)
+                    if j == 1:
+                        quantize(w1_codes[1], w1_scales[1], w1_words[1])
+                        widen(1, 1)
+                    if j == 2:
+                        widen(1, 2)
+                        widen(1, 3)
+                    if j == 5:
+                        turn_w2(0)
+                        turn_w2(1)
+                    if j == 6:
+                        unbank("v", w2_words, 0, banks.pop(("w2", 0)))
+                        unbank("s", w2_words, 1, banks.pop(("w2", 1)))
+                if j == 0:
+                    if nxt:
+                        make_c("s", i + 1, 0)
+                    if prev:
+                        relu("v", i - 1, 1)
+                if j == 1:
+                    if nxt:
+                        make_c("s", i + 1, 1)
+                    if prev:
+                        quant_h(i - 1, 1)
+                    if i == 1:
+                        quantize(w2_codes, w2_scales, w2_words)
+                if j == 2:
+                    relu("s", i, 0, 0, 256)
+                if j in (2, 3) and i + 2 < TILES:
+                    widen(i + 2, 2 * (j - 2))
+                    widen(i + 2, 2 * (j - 2) + 1)
+                if j == 3:
+                    if nxt:
+                        turn_x(i + 1, 0)
+                        turn_x(i + 1, 1)
+                        copy_x("s", i + 1, 0)
+                        copy_x("s", i + 1, 1)
+                        make_c("s", i + 1, 2)
+                    if prev:
+                        layer2(i - 1)
+                        tanh(i - 1, 0)
+                        tanh(i - 1, 1)
+                if j == 4:
+                    relu("v", i, 0, 256, TOK)
+                    if nxt:
+                        make_c("s", i + 1, 3)
+                if j == 5:
+                    quant_h(i, 0)
+                    if nxt:
+                        make_c("s", i + 1, 4)
+                if j == 6:
+                    if nxt:
+                        quant_x(i + 1)
+                        make_c("s", i + 1, 5)
+                    else:
+                        relu("v", i, 1, 0, 256)
+                if j == 7:
+                    if prev:
+                        turn_out(i - 1, 0)
+                        turn_out(i - 1, 1)
+                        store("s", i - 1, 0)
+                        store("s", i - 1, 1)
+                    if not nxt:
+                        quant_h(i, 1, 0, 256)
+                        layer2_half(i, 0)
+                        tanh_half(i, 0)
+                    if nxt:
+                        make_c("s", i + 1, 6)
+                        make_c("s", i + 1, 7)
+
+        relu("v", last, 1, 256, TOK)
+        quant_h(last, 1, 256, TOK)
+        layer2_half(last, 1)
+        tanh_half(last, 1)
+        turn_out(last, 0)
+        turn_out(last, 1)
+        store("v", last, 0)
+        store("v", last, 1)

@@ -22,7 +22,7 @@ FLOPS = 2 * E * (D + 1) * MID + 2 * E * MID * OUT
 TOK = 512
 TILES = E // TOK
 SUBS = TOK // P
-ROW = 544
+SHARED = (7,)
 
 
 def tile_edgenetwork_t_kernel(tc, dst_feat, dst_hidden, src_feat, src_bytes, src_scale,
@@ -44,8 +44,9 @@ def tile_edgenetwork_t_kernel(tc, dst_feat, dst_hidden, src_feat, src_bytes, src
         edge_bc = [keep.tile([P, TOK], BF16, name=f"edge_bc{i}") for i in range(TILES)]
         x_rows = [keep.tile([P, SUBS, D], BF16, name=f"x_rows{i}", align_bytes=64) for i in range(TILES)]
         x_bytes = [keep.tile([P, SUBS, H], U8, name=f"x_bytes{i}", align_bytes=64) for i in range(TILES)]
-        w1_rows = [keep.tile([P, 4, ROW], BF16, name=f"w1_rows{h}", align_bytes=64) for h in range(2)]
+        w1_rows = [keep.tile([P, 4, D], BF16, name=f"w1_rows{h}", align_bytes=64) for h in range(2)]
         w2_rows = keep.tile([P, 2, MID], BF16, name="w2_rows", align_bytes=64)
+        w_bf = [keep.tile([P, 4, 2], BF16, name=f"w_bf{h}") for h in range(2)]
         b1_bf = keep.tile([P, 2, 4], BF16, name="b1_bf")
         b2_bf = keep.tile([P, 2], BF16, name="b2_bf")
 
@@ -62,17 +63,22 @@ def tile_edgenetwork_t_kernel(tc, dst_feat, dst_hidden, src_feat, src_bytes, src
             nc.sync.dma_start(out=edge_bc[i][:], in_=edge[TOK * i:TOK * (i + 1)].partition_broadcast(P))
 
         def load_w1(h):
-            nc.sync.dma_start(out=w1_rows[h][:, :, 0:D + 1],
-                              in_=w1[512 * h:512 * (h + 1), :].rearrange("(p t) k -> p t k", t=4))
+            nc.sync.dma_start(out=w1_rows[h][:],
+                              in_=w1[512 * h:512 * (h + 1), 0:D].rearrange("(p t) k -> p t k", t=4))
 
+        with nc.allow_non_contiguous_dma(reason="one bfloat16 of each row of W1"):
+            for h in range(2):
+                nc.gpsimd.dma_start(out=w_bf[h][:, :, 0:1],
+                                    in_=w1[512 * h:512 * (h + 1), D:D + 1].rearrange("(p t) o -> p t o", t=4))
+                if h == 0:
+                    nc.gpsimd.dma_start(out=b1_bf[:], in_=b1.rearrange("(h p t) -> p h t", h=2, t=4))
+        load_edge(0)
         nc.sync.dma_start(out=scale_bc[:], in_=src_scale.rearrange("o k -> (o k)").partition_broadcast(P))
         load_x(0)
         load_w1(0)
-        nc.sync.dma_start(out=b1_bf[:], in_=b1.rearrange("(h p t) -> p h t", h=2, t=4))
-        load_edge(0)
+        load_edge(1)
         load_w1(1)
         load_x(1)
-        load_edge(1)
         nc.sync.dma_start(out=w2_rows[:], in_=w2.rearrange("(p c) k -> p c k", c=2))
         nc.sync.dma_start(out=b2_bf[:], in_=b2.rearrange("(p c) -> p c", c=2))
         for i in range(2, TILES):
@@ -89,9 +95,9 @@ def tile_edgenetwork_t_kernel(tc, dst_feat, dst_hidden, src_feat, src_bytes, src
         w2_codes = keep.tile([P, 512], U32, name="w2_codes", align_bytes=64)
         w2_scales = keep.tile([P, 512], U8, name="w2_scales", align_bytes=64)
 
-        def quantize(codes, scales, words):
-            nc.vector.quantize_mx(out=codes[:].bitcast(FP8X4), scales=scales[:],
-                                  in_=words[:].rearrange("p n u -> p (n u)").bitcast(BF16))
+        def quantize(codes, scales, words, lo=0, hi=512):
+            nc.vector.quantize_mx(out=codes[:, lo:hi].bitcast(FP8X4), scales=scales[:, lo:hi],
+                                  in_=words[:, lo:hi, :].rearrange("p n u -> p (n u)").bitcast(BF16))
 
         def bank4():
             return psum.tile([P, 2, 2, P], F32, name="turned", bufs=2)
@@ -137,11 +143,10 @@ def tile_edgenetwork_t_kernel(tc, dst_feat, dst_hidden, src_feat, src_bytes, src
         cs = {}
 
         def make_c(eng, i, ht):
-            if i not in cs:
-                ct = work.tile([P, 8, TOK], F32, name="edge_term")
-                cs[i] = ct
+            ct = work.tile([P, TOK], F32, name="edge_term", bufs=18)
+            cs[i, ht] = ct
             h, t = ht // 4, ht % 4
-            o, w_ap, b_ap = cs[i][:, ht, :], w_col[:, h, t:t + 1], b1_col[:, h, t:t + 1]
+            o, w_ap, b_ap = ct[:], w_col[:, h, t:t + 1], b1_col[:, h, t:t + 1]
             if eng == "s":
                 nc.scalar.activation(out=o, in_=edge_bc[i][:], func=ACT.Identity, scale=w_ap, bias=b_ap)
             elif eng == "v":
@@ -149,35 +154,34 @@ def tile_edgenetwork_t_kernel(tc, dst_feat, dst_hidden, src_feat, src_bytes, src
             else:
                 nc.gpsimd.tensor_scalar(out=o, in0=edge_bc[i][:], scalar1=w_ap, scalar2=b_ap, op0=MULT, op1=ADD)
 
-        mm, hb, hc, hs = {}, {}, {}, {}
+        mm, hp, hb, hc, hs = {}, {}, {}, {}, {}
 
         def layer1(i, j):
-            h, s = j // 4, j % 4
-            acc = psum.tile([P, 4, P], F32, name="acc", bufs=4)
-            for t in range(4):
-                nc.tensor.matmul_mx(out=acc[:, t, :],
-                                    lhsT=w1_codes[h][:, P * t:P * (t + 1)].bitcast(FP8X4),
-                                    lhsT_scale=w1_scales[h][:, P * t:P * (t + 1)],
-                                    rhs=xc[i][:, P * s:P * (s + 1)].bitcast(FP8X4),
-                                    rhs_scale=xs[i][:, P * s:P * (s + 1)], start=True, stop=True)
+            h, t = j // 4, j % 4
+            acc = psum.tile([P, TOK], F32, name="acc", bufs=4)
+            nc.tensor.matmul_mx(out=acc[:],
+                                lhsT=w1_codes[h][:, P * t:P * (t + 1)].bitcast(FP8X4),
+                                lhsT_scale=w1_scales[h][:, P * t:P * (t + 1)],
+                                rhs=xc[i][:].bitcast(FP8X4), rhs_scale=xs[i][:], start=True, stop=True)
             mm[i, j] = acc
 
         def add(i, j):
-            h, s = j // 4, j % 4
-            if s == 0:
+            h, t = j // 4, j % 4
+            if t == 0:
+                pt = work.tile([P, 4, TOK], BF16, name="planes", bufs=3, align_bytes=64)
+                hp[i, h] = pt
+            nc.vector.tensor_tensor(out=hp[i, h][:, t, :], in0=mm.pop((i, j))[:], in1=cs.pop((i, j))[:], op=ADD)
+
+        def relu(eng, i, h, lo, hi):
+            if (i, h) not in hb:
                 ht = work.tile([P, TOK, 4], BF16, name="hidden", bufs=3, align_bytes=64)
                 hb[i, h] = ht
-            nc.vector.tensor_tensor(out=hb[i, h][:, P * s:P * (s + 1), :],
-                                    in0=mm.pop((i, j))[:].rearrange("p t n -> p n t"),
-                                    in1=cs[i][:, 4 * h:4 * (h + 1), P * s:P * (s + 1)].rearrange("p t n -> p n t"),
-                                    op=ADD)
-
-        def relu(eng, i, h, lo=0, hi=TOK):
-            part = hb[i, h][:, lo:hi, :]
+            dst = hb[i, h][:, lo:hi, :].rearrange("p (c i) t -> p c t i", i=4)
+            part = hp[i, h][:, :, lo:hi].rearrange("p t (c i) -> p c t i", i=4)
             if eng == "s":
-                nc.scalar.activation(out=part, in_=part, func=ACT.Relu)
+                nc.scalar.activation(out=dst, in_=part, func=ACT.Relu)
             else:
-                nc.vector.tensor_scalar_max(out=part, in0=part, scalar1=0.0)
+                nc.vector.tensor_scalar_max(out=dst, in0=part, scalar1=0.0)
 
         def quant_h(i, h, lo=0, hi=TOK):
             if lo == 0:
@@ -252,117 +256,122 @@ def tile_edgenetwork_t_kernel(tc, dst_feat, dst_hidden, src_feat, src_bytes, src
             banks["w2", h] = bank
             turn(bank, [w2_rows[:, c, 512 * h:512 * (h + 1)].bitcast(F32) for c in range(2)])
 
+        nc.gpsimd.tensor_copy(out=w_col[:, 0, :], in_=w_bf[0][:, :, 0])
         nc.gpsimd.tensor_copy(out=b1_col[:], in_=b1_bf[:])
-        nc.gpsimd.tensor_copy(out=w_col[:, 0, :], in_=w1_rows[0][:, :, D])
-        nc.gpsimd.tensor_copy(out=w_col[:, 1, :], in_=w1_rows[1][:, :, D])
+        nc.gpsimd.tensor_copy(out=w_col[:, 1, :], in_=w_bf[1][:, :, 0])
         nc.gpsimd.tensor_copy(out=b2_col[:], in_=b2_bf[:])
 
+        for t in range(3):
+            make_c("s", 0, t)
         for s in range(4):
             widen(0, s)
+        for t in range(3, 8):
+            make_c("v", 0, t)
         turn_x(0, 0)
         turn_x(0, 1)
         copy_x("v", 0, 0)
         copy_x("s", 0, 1)
         turn_w1(0, 0)
         turn_w1(0, 1)
-        quant_x(0)
         unbank("s", w1_words[0], 0, banks.pop(("w", 0, 0)))
-        unbank("v", w1_words[0], 1, banks.pop(("w", 0, 1)))
-        make_c("s", 0, 0)
-        make_c("v", 0, 2)
-        quantize(w1_codes[0], w1_scales[0], w1_words[0])
-        make_c("v", 0, 3)
-        make_c("s", 0, 1)
+        quant_x(0)
+        quantize(w1_codes[0], w1_scales[0], w1_words[0], 0, 256)
+        unbank("s", w1_words[0], 1, banks.pop(("w", 0, 1)))
+        make_c("s", 1, 0)
         turn_w1(1, 0)
-        turn_w1(1, 1)
         unbank("s", w1_words[1], 0, banks.pop(("w", 1, 0)))
+        layer1(0, 0)
+        layer1(0, 1)
+        turn_w1(1, 1)
+        unbank("s", w1_words[1], 1, banks.pop(("w", 1, 1)))
+        for t in range(1, 4):
+            make_c("s", 1, t)
+        quantize(w1_codes[0], w1_scales[0], w1_words[0], 256, 512)
 
         last = TILES - 1
         for i in range(TILES):
             nxt = i < last
             prev = i > 0
             for j in range(8):
-                layer1(i, j)
+                if j < 6:
+                    layer1(i, j + 2)
+                elif nxt:
+                    layer1(i + 1, j - 6)
                 add(i, j)
                 if i == 0:
                     if j == 0:
-                        unbank("v", w1_words[1], 1, banks.pop(("w", 1, 1)))
-                        for t in range(4, 8):
-                            make_c("s", 0, t)
                         widen(1, 0)
-                    if j == 1:
-                        quantize(w1_codes[1], w1_scales[1], w1_words[1])
                         widen(1, 1)
-                    if j == 2:
+                    if j == 1:
+                        quantize(w1_codes[1], w1_scales[1], w1_words[1], 0, 256)
                         widen(1, 2)
                         widen(1, 3)
+                    if j == 2:
+                        quantize(w1_codes[1], w1_scales[1], w1_words[1], 256, 512)
                     if j == 5:
                         turn_w2(0)
                         turn_w2(1)
-                    if j == 6:
-                        unbank("v", w2_words, 0, banks.pop(("w2", 0)))
-                        unbank("s", w2_words, 1, banks.pop(("w2", 1)))
+                    if j == 7:
+                        unbank("s", w2_words, 0, banks.pop(("w2", 0)))
+                        unbank("v", w2_words, 1, banks.pop(("w2", 1)))
+                if i == 1 and j == 1:
+                    quantize(w2_codes, w2_scales, w2_words)
                 if j == 0:
-                    if nxt:
-                        make_c("s", i + 1, 0)
                     if prev:
-                        relu("v", i - 1, 1)
+                        relu("s" if i in SHARED else "v", i - 1, 1, 0, 256)
+                    if nxt:
+                        make_c("s", i + 1, 4)
                 if j == 1:
                     if nxt:
-                        make_c("s", i + 1, 1)
+                        make_c("s", i + 1, 5)
+                    if prev:
+                        relu("v", i - 1, 1, 256, TOK)
+                if j == 2:
                     if prev:
                         quant_h(i - 1, 1)
-                    if i == 1:
-                        quantize(w2_codes, w2_scales, w2_words)
-                if j == 2:
-                    relu("s", i, 0, 0, 256)
-                if j in (2, 3) and i + 2 < TILES:
-                    widen(i + 2, 2 * (j - 2))
-                    widen(i + 2, 2 * (j - 2) + 1)
-                if j == 3:
                     if nxt:
                         turn_x(i + 1, 0)
                         turn_x(i + 1, 1)
                         copy_x("s", i + 1, 0)
                         copy_x("s", i + 1, 1)
-                        make_c("s", i + 1, 2)
+                if j in (3, 4) and i + 2 < TILES:
+                    widen(i + 2, 2 * (j - 3))
+                    widen(i + 2, 2 * (j - 3) + 1)
+                if j == 3:
+                    if nxt:
+                        make_c("s", i + 1, 6)
                     if prev:
                         layer2(i - 1)
+                if j == 4:
+                    if prev:
                         tanh(i - 1, 0)
                         tanh(i - 1, 1)
-                if j == 4:
-                    relu("v", i, 0, 256, TOK)
                     if nxt:
-                        make_c("s", i + 1, 3)
+                        make_c("s", i + 1, 7)
                 if j == 5:
-                    quant_h(i, 0)
-                    if nxt:
-                        make_c("s", i + 1, 4)
-                if j == 6:
+                    relu("s", i, 0, 0, 256)
                     if nxt:
                         quant_x(i + 1)
-                        make_c("s", i + 1, 5)
-                    else:
-                        relu("v", i, 1, 0, 256)
-                if j == 7:
                     if prev:
                         turn_out(i - 1, 0)
                         turn_out(i - 1, 1)
+                if j == 6:
+                    relu("v" if nxt else "s", i, 0, 256, TOK)
+                    if prev:
                         store("s", i - 1, 0)
                         store("s", i - 1, 1)
-                    if not nxt:
-                        quant_h(i, 1, 0, 256)
-                        layer2_half(i, 0)
-                        tanh_half(i, 0)
-                    if nxt:
-                        make_c("s", i + 1, 6)
-                        make_c("s", i + 1, 7)
+                if j == 7:
+                    quant_h(i, 0)
+                    if i + 2 < TILES:
+                        for t in range(4):
+                            make_c("s", i + 2, t)
 
-        relu("v", last, 1, 256, TOK)
-        quant_h(last, 1, 256, TOK)
-        layer2_half(last, 1)
-        tanh_half(last, 1)
-        turn_out(last, 0)
-        turn_out(last, 1)
-        store("v", last, 0)
-        store("v", last, 1)
+        for half in range(2):
+            relu("vs"[half], last, 1, 256 * half, 256 * (half + 1))
+        for half in range(2):
+            quant_h(last, 1, 256 * half, 256 * (half + 1))
+            layer2_half(last, half)
+            tanh_half(last, half)
+        for half in range(2):
+            turn_out(last, half)
+            store("v", last, half)

@@ -22,7 +22,9 @@ FLOPS = 2 * E * (D + 1) * MID + 2 * E * MID * OUT
 TOK = 512
 TILES = E // TOK
 SUBS = TOK // P
-SHARED = (7,)
+RELU_S = 0
+RELU_S0 = 0
+GC = "gg"
 
 
 def tile_edgenetwork_t_kernel(tc, dst_feat, dst_hidden, src_feat, src_bytes, src_scale,
@@ -38,7 +40,6 @@ def tile_edgenetwork_t_kernel(tc, dst_feat, dst_hidden, src_feat, src_bytes, src
         make_identity(nc, ident[:])
         warm = keep.tile([P, 1], F32, name="warm")
         nc.vector.memset(warm[:], 0.0)
-        nc.scalar.activation(out=warm[:], in_=warm[:], func=ACT.Tanh)
 
         scale_bc = keep.tile([P, H], F32, name="scale_bc")
         edge_bc = [keep.tile([P, TOK], BF16, name=f"edge_bc{i}") for i in range(TILES)]
@@ -50,14 +51,14 @@ def tile_edgenetwork_t_kernel(tc, dst_feat, dst_hidden, src_feat, src_bytes, src
         b1_bf = keep.tile([P, 2, 4], BF16, name="b1_bf")
         b2_bf = keep.tile([P, 2], BF16, name="b2_bf")
 
-        def rows(ap, i):
-            return ap[TOK * i:TOK * (i + 1), :].rearrange("(s p) f -> p s f", p=P)
+        def load_x(i, s0=0, s1=SUBS):
+            def rows(ap):
+                return ap[TOK * i + P * s0:TOK * i + P * s1, :].rearrange("(s p) f -> p s f", p=P)
 
-        def load_x(i):
-            nc.sync.dma_start(out=x_bytes[i][:], in_=rows(src_bytes, i))
-            nc.sync.dma_start(out=x_rows[i][:, :, 0:F], in_=rows(dst_feat, i))
-            nc.sync.dma_start(out=x_rows[i][:, :, F:F + H], in_=rows(dst_hidden, i))
-            nc.sync.dma_start(out=x_rows[i][:, :, F + H:2 * F + H], in_=rows(src_feat, i))
+            nc.sync.dma_start(out=x_bytes[i][:, s0:s1, :], in_=rows(src_bytes))
+            nc.sync.dma_start(out=x_rows[i][:, s0:s1, 0:F], in_=rows(dst_feat))
+            nc.sync.dma_start(out=x_rows[i][:, s0:s1, F:F + H], in_=rows(dst_hidden))
+            nc.sync.dma_start(out=x_rows[i][:, s0:s1, F + H:2 * F + H], in_=rows(src_feat))
 
         def load_edge(i):
             nc.sync.dma_start(out=edge_bc[i][:], in_=edge[TOK * i:TOK * (i + 1)].partition_broadcast(P))
@@ -68,14 +69,16 @@ def tile_edgenetwork_t_kernel(tc, dst_feat, dst_hidden, src_feat, src_bytes, src
 
         with nc.allow_non_contiguous_dma(reason="one bfloat16 of each row of W1"):
             for h in range(2):
-                nc.gpsimd.dma_start(out=w_bf[h][:, :, 0:1],
+                nc.scalar.dma_start(out=w_bf[h][:, :, 0:1],
                                     in_=w1[512 * h:512 * (h + 1), D:D + 1].rearrange("(p t) o -> p t o", t=4))
                 if h == 0:
-                    nc.gpsimd.dma_start(out=b1_bf[:], in_=b1.rearrange("(h p t) -> p h t", h=2, t=4))
+                    nc.scalar.dma_start(out=b1_bf[:], in_=b1.rearrange("(h p t) -> p h t", h=2, t=4))
+        nc.scalar.activation(out=warm[:], in_=warm[:], func=ACT.Tanh)
         load_edge(0)
         nc.sync.dma_start(out=scale_bc[:], in_=src_scale.rearrange("o k -> (o k)").partition_broadcast(P))
-        load_x(0)
+        load_x(0, 0, 2)
         load_w1(0)
+        load_x(0, 2, SUBS)
         load_edge(1)
         load_w1(1)
         load_x(1)
@@ -123,30 +126,39 @@ def tile_edgenetwork_t_kernel(tc, dst_feat, dst_hidden, src_feat, src_bytes, src
             nc.vector.tensor_tensor(out=x_rows[i][:, s, 2 * F + H:D], in0=x_bytes[i][:, s, :].bitcast(FP8),
                                     in1=scale_bc[:], op=MULT)
 
+        def widen_off_vector(i):
+            wide = work.tile([P, SUBS, H], BF16, name="wide")
+            nc.scalar.copy(out=wide[:].rearrange("p s f -> p (s f)"),
+                           in_=x_bytes[i][:].rearrange("p s f -> p (s f)").bitcast(FP8))
+            for s in range(SUBS):
+                nc.gpsimd.tensor_tensor(out=x_rows[i][:, s, 2 * F + H:D], in0=wide[:, s, :], in1=scale_bc[:], op=MULT)
+
         def turn_x(i, half):
             bank = bank4()
             banks[i, half] = bank
             turn(bank, [x_rows[i][:, 2 * half + a, :].bitcast(F32) for a in range(2)])
 
         def copy_x(eng, i, half):
-            if half == 0:
+            if i not in xw:
                 xt = work.tile([P, TOK, 2], F32, name="x_words", align_bytes=64)
                 xw[i] = xt
             unbank(eng, xw[i], half, banks.pop((i, half)))
 
-        def quant_x(i):
-            codes = work.tile([P, TOK], U32, name="x_codes", align_bytes=64)
-            scales = work.tile([P, TOK], U8, name="x_scales", align_bytes=64)
-            quantize(codes, scales, xw[i])
-            xc[i], xs[i] = codes, scales
+        def quant_x(i, lo=0, hi=TOK):
+            if lo == 0:
+                codes = work.tile([P, TOK], U32, name="x_codes", bufs=3, align_bytes=64)
+                scales = work.tile([P, TOK], U8, name="x_scales", bufs=3, align_bytes=64)
+                xc[i], xs[i] = codes, scales
+            quantize(xc[i], xs[i], xw[i], lo, hi)
 
         cs = {}
 
         def make_c(eng, i, ht):
-            ct = work.tile([P, TOK], F32, name="edge_term", bufs=18)
-            cs[i, ht] = ct
+            if i not in cs:
+                ct = work.tile([P, 8, TOK], F32, name="edge_term", bufs=3)
+                cs[i] = ct
             h, t = ht // 4, ht % 4
-            o, w_ap, b_ap = ct[:], w_col[:, h, t:t + 1], b1_col[:, h, t:t + 1]
+            o, w_ap, b_ap = cs[i][:, ht, :], w_col[:, h, t:t + 1], b1_col[:, h, t:t + 1]
             if eng == "s":
                 nc.scalar.activation(out=o, in_=edge_bc[i][:], func=ACT.Identity, scale=w_ap, bias=b_ap)
             elif eng == "v":
@@ -154,34 +166,34 @@ def tile_edgenetwork_t_kernel(tc, dst_feat, dst_hidden, src_feat, src_bytes, src
             else:
                 nc.gpsimd.tensor_scalar(out=o, in0=edge_bc[i][:], scalar1=w_ap, scalar2=b_ap, op0=MULT, op1=ADD)
 
-        mm, hp, hb, hc, hs = {}, {}, {}, {}, {}
+        mm, hb, hc, hs = {}, {}, {}, {}
 
-        def layer1(i, j):
-            h, t = j // 4, j % 4
-            acc = psum.tile([P, TOK], F32, name="acc", bufs=4)
-            nc.tensor.matmul_mx(out=acc[:],
-                                lhsT=w1_codes[h][:, P * t:P * (t + 1)].bitcast(FP8X4),
-                                lhsT_scale=w1_scales[h][:, P * t:P * (t + 1)],
-                                rhs=xc[i][:].bitcast(FP8X4), rhs_scale=xs[i][:], start=True, stop=True)
-            mm[i, j] = acc
+        def layer1(i, h, s):
+            acc = psum.tile([P, 4, P], F32, name="acc", bufs=4)
+            for t in range(4):
+                nc.tensor.matmul_mx(out=acc[:, t, :],
+                                    lhsT=w1_codes[h][:, P * t:P * (t + 1)].bitcast(FP8X4),
+                                    lhsT_scale=w1_scales[h][:, P * t:P * (t + 1)],
+                                    rhs=xc[i][:, P * s:P * (s + 1)].bitcast(FP8X4),
+                                    rhs_scale=xs[i][:, P * s:P * (s + 1)], start=True, stop=True)
+            mm[i, h, s] = acc
 
-        def add(i, j):
-            h, t = j // 4, j % 4
-            if t == 0:
-                pt = work.tile([P, 4, TOK], BF16, name="planes", bufs=3, align_bytes=64)
-                hp[i, h] = pt
-            nc.vector.tensor_tensor(out=hp[i, h][:, t, :], in0=mm.pop((i, j))[:], in1=cs.pop((i, j))[:], op=ADD)
+        def add(i, h, s):
+            if (i, h) not in hb:
+                ht = work.tile([P, TOK, 4], BF16, name="hidden", bufs=4, align_bytes=64)
+                hb[i, h] = ht
+            cols = slice(P * s, P * (s + 1))
+            nc.vector.tensor_tensor(out=hb[i, h][:, cols, :].rearrange("p (c i) t -> p c t i", i=4),
+                                    in0=mm.pop((i, h, s))[:].rearrange("p t (c i) -> p c t i", i=4),
+                                    in1=cs[i][:, 4 * h:4 * (h + 1), cols].rearrange("p t (c i) -> p c t i", i=4),
+                                    op=ADD)
 
         def relu(eng, i, h, lo, hi):
-            if (i, h) not in hb:
-                ht = work.tile([P, TOK, 4], BF16, name="hidden", bufs=3, align_bytes=64)
-                hb[i, h] = ht
-            dst = hb[i, h][:, lo:hi, :].rearrange("p (c i) t -> p c t i", i=4)
-            part = hp[i, h][:, :, lo:hi].rearrange("p t (c i) -> p c t i", i=4)
+            part = hb[i, h][:, lo:hi, :].rearrange("p n t -> p (n t)")
             if eng == "s":
-                nc.scalar.activation(out=dst, in_=part, func=ACT.Relu)
+                nc.scalar.activation(out=part, in_=part, func=ACT.Relu)
             else:
-                nc.vector.tensor_scalar_max(out=dst, in0=part, scalar1=0.0)
+                nc.vector.tensor_scalar_max(out=part, in0=part, scalar1=0.0)
 
         def quant_h(i, h, lo=0, hi=TOK):
             if lo == 0:
@@ -214,8 +226,8 @@ def tile_edgenetwork_t_kernel(tc, dst_feat, dst_hidden, src_feat, src_bytes, src
                                         lhsT=w2_codes[:, w0:w0 + P].bitcast(FP8X4), lhsT_scale=w2_scales[:, w0:w0 + P],
                                         rhs=hc[i, h][:, n0:n0 + 256].bitcast(FP8X4), rhs_scale=hs[i, h][:, n0:n0 + 256],
                                         start=(h == 0), stop=(h == 1))
-            if half == 0:
-                ot = work.tile([P, 2, TOK], F32, name="channels")
+            if i not in ob:
+                ot = work.tile([P, 2, TOK], F32, name="channels", bufs=3)
                 ob[i] = ot
             l2[i, half] = acc2
 
@@ -226,8 +238,8 @@ def tile_edgenetwork_t_kernel(tc, dst_feat, dst_hidden, src_feat, src_bytes, src
                                      func=ACT.Tanh, bias=b2_col[:, c:c + 1])
 
         def tanh(i, c):
-            if c == 0:
-                ot = work.tile([P, 2, TOK], F32, name="channels")
+            if i not in ob:
+                ot = work.tile([P, 2, TOK], F32, name="channels", bufs=3)
                 ob[i] = ot
             nc.scalar.activation(out=ob[i][:, c, :], in_=l2.pop((i, c))[:], func=ACT.Tanh, bias=b2_col[:, c:c + 1])
 
@@ -256,122 +268,139 @@ def tile_edgenetwork_t_kernel(tc, dst_feat, dst_hidden, src_feat, src_bytes, src
             banks["w2", h] = bank
             turn(bank, [w2_rows[:, c, 512 * h:512 * (h + 1)].bitcast(F32) for c in range(2)])
 
-        nc.gpsimd.tensor_copy(out=w_col[:, 0, :], in_=w_bf[0][:, :, 0])
-        nc.gpsimd.tensor_copy(out=b1_col[:], in_=b1_bf[:])
-        nc.gpsimd.tensor_copy(out=w_col[:, 1, :], in_=w_bf[1][:, :, 0])
+        nc.vector.tensor_copy(out=w_col[:, 0, :], in_=w_bf[0][:, :, 0])
+        nc.vector.tensor_copy(out=b1_col[:], in_=b1_bf[:])
+        nc.vector.tensor_copy(out=w_col[:, 1, :], in_=w_bf[1][:, :, 0])
         nc.gpsimd.tensor_copy(out=b2_col[:], in_=b2_bf[:])
 
         for t in range(3):
             make_c("s", 0, t)
-        for s in range(4):
-            widen(0, s)
+        widen(0, 0)
+        widen(0, 1)
         for t in range(3, 8):
             make_c("v", 0, t)
         turn_x(0, 0)
-        turn_x(0, 1)
-        copy_x("v", 0, 0)
-        copy_x("s", 0, 1)
+        copy_x("s", 0, 0)
         turn_w1(0, 0)
-        turn_w1(0, 1)
+        quant_x(0, 0, 256)
         unbank("s", w1_words[0], 0, banks.pop(("w", 0, 0)))
-        quant_x(0)
-        quantize(w1_codes[0], w1_scales[0], w1_words[0], 0, 256)
-        unbank("s", w1_words[0], 1, banks.pop(("w", 0, 1)))
-        make_c("s", 1, 0)
+        turn_w1(0, 1)
+        unbank("v", w1_words[0], 1, banks.pop(("w", 0, 1)))
+        quantize(w1_codes[0], w1_scales[0], w1_words[0])
+        widen(0, 2)
+        widen(0, 3)
+        last = TILES - 1
+        steps = [(i, g) for i in range(TILES) for g in range(4)]
+
+        def layer1_step(i, g):
+            for s in (2 * (g % 2), 2 * (g % 2) + 1):
+                layer1(i, g // 2, s)
+
+        def add_step(i, g):
+            for s in (2 * (g % 2) + 1, 2 * (g % 2)):
+                add(i, g // 2, s)
+
+        layer1_step(0, 0)
+        turn_x(0, 1)
+        copy_x("s", 0, 1)
         turn_w1(1, 0)
         unbank("s", w1_words[1], 0, banks.pop(("w", 1, 0)))
-        layer1(0, 0)
-        layer1(0, 1)
+        make_c("s", 1, 0)
+        add_step(0, 0)
+        quant_x(0, 256, TOK)
+        layer1_step(0, 1)
         turn_w1(1, 1)
         unbank("s", w1_words[1], 1, banks.pop(("w", 1, 1)))
         for t in range(1, 4):
             make_c("s", 1, t)
-        quantize(w1_codes[0], w1_scales[0], w1_words[0], 256, 512)
-
-        last = TILES - 1
-        for i in range(TILES):
+        for s in range(SUBS):
+            widen(1, s)
+        add_step(0, 1)
+        quantize(w1_codes[1], w1_scales[1], w1_words[1])
+        layer1_step(0, 2)
+        for n, (i, g) in enumerate(steps):
             nxt = i < last
             prev = i > 0
-            for j in range(8):
-                if j < 6:
-                    layer1(i, j + 2)
-                elif nxt:
-                    layer1(i + 1, j - 6)
-                add(i, j)
+            if n > 1:
+                if n + 1 < len(steps):
+                    layer1_step(*steps[n + 1])
+                add_step(i, g)
+            if g == 0:
+                if prev:
+                    relu("v", i - 1, 1, RELU_S, TOK)
+                if prev and nxt:
+                    copy_x("s", i + 1, 1)
+                    copy_x("s", i + 1, 0)
                 if i == 0:
-                    if j == 0:
-                        widen(1, 0)
-                        widen(1, 1)
-                    if j == 1:
-                        quantize(w1_codes[1], w1_scales[1], w1_words[1], 0, 256)
-                        widen(1, 2)
-                        widen(1, 3)
-                    if j == 2:
-                        quantize(w1_codes[1], w1_scales[1], w1_words[1], 256, 512)
-                    if j == 5:
-                        turn_w2(0)
-                        turn_w2(1)
-                    if j == 7:
-                        unbank("s", w2_words, 0, banks.pop(("w2", 0)))
-                        unbank("v", w2_words, 1, banks.pop(("w2", 1)))
-                if i == 1 and j == 1:
-                    quantize(w2_codes, w2_scales, w2_words)
-                if j == 0:
-                    if prev:
-                        relu("s" if i in SHARED else "v", i - 1, 1, 0, 256)
-                    if nxt:
-                        make_c("s", i + 1, 4)
-                if j == 1:
-                    if nxt:
-                        make_c("s", i + 1, 5)
-                    if prev:
-                        relu("v", i - 1, 1, 256, TOK)
-                if j == 2:
-                    if prev:
-                        quant_h(i - 1, 1)
-                    if nxt:
-                        turn_x(i + 1, 0)
-                        turn_x(i + 1, 1)
-                        copy_x("s", i + 1, 0)
-                        copy_x("s", i + 1, 1)
-                if j in (3, 4) and i + 2 < TILES:
-                    widen(i + 2, 2 * (j - 3))
-                    widen(i + 2, 2 * (j - 3) + 1)
-                if j == 3:
-                    if nxt:
-                        make_c("s", i + 1, 6)
-                    if prev:
-                        layer2(i - 1)
-                if j == 4:
-                    if prev:
-                        tanh(i - 1, 0)
-                        tanh(i - 1, 1)
-                    if nxt:
-                        make_c("s", i + 1, 7)
-                if j == 5:
-                    relu("s", i, 0, 0, 256)
+                    turn_x(1, 0)
+                    turn_x(1, 1)
+                if nxt:
+                    make_c("s", i + 1, 4)
+                    make_c("s", i + 1, 5)
+            if g == 1:
+                if i > 1:
+                    turn_out(i - 2, 0)
+                    turn_out(i - 2, 1)
+                if i == 1:
+                    turn_w2(0)
+                    turn_w2(1)
+                if RELU_S0:
+                    relu("s", i, 0, 0, RELU_S0)
+                if prev:
+                    quant_h(i - 1, 1)
                     if nxt:
                         quant_x(i + 1)
-                    if prev:
-                        turn_out(i - 1, 0)
-                        turn_out(i - 1, 1)
-                if j == 6:
-                    relu("v" if nxt else "s", i, 0, 256, TOK)
-                    if prev:
-                        store("s", i - 1, 0)
-                        store("s", i - 1, 1)
-                if j == 7:
-                    quant_h(i, 0)
-                    if i + 2 < TILES:
-                        for t in range(4):
-                            make_c("s", i + 2, t)
+                else:
+                    for s in range(SUBS):
+                        widen(2, s)
+                    copy_x("s", 1, 1)
+                    copy_x("s", 1, 0)
+                if i > 1:
+                    store("s", i - 2, 1)
+                    store("s", i - 2, 0)
+                if nxt:
+                    make_c(GC[0], i + 1, 6)
+                    make_c(GC[1], i + 1, 7)
+                if i == 1:
+                    unbank("s", w2_words, 1, banks.pop(("w2", 1)))
+                    unbank("s", w2_words, 0, banks.pop(("w2", 0)))
+            if g == 2:
+                relu("v", i, 0, RELU_S0, TOK)
+                if i + 3 < TILES:
+                    widen_off_vector(i + 3)
+                if i == 1:
+                    quantize(w2_codes, w2_scales, w2_words)
+                if prev:
+                    layer2(i - 1)
+                if i == 0:
+                    quant_x(1)
+                if i + 2 < TILES:
+                    make_c("s", i + 2, 0)
+                    make_c("s", i + 2, 1)
+            if g == 3:
+                quant_h(i, 0)
+                if prev:
+                    tanh(i - 1, 1)
+                    tanh(i - 1, 0)
+                if i + 2 < TILES:
+                    turn_x(i + 2, 0)
+                    turn_x(i + 2, 1)
+                if nxt and RELU_S:
+                    relu("s", i, 1, 0, RELU_S)
+                if i + 2 < TILES:
+                    make_c("s", i + 2, 2)
+                    make_c("s", i + 2, 3)
 
+        relu("v", last, 1, 0, 256)
+        relu("s", last, 1, 256, TOK)
         for half in range(2):
-            relu("vs"[half], last, 1, 256 * half, 256 * (half + 1))
+            turn_out(last - 1, half)
         for half in range(2):
             quant_h(last, 1, 256 * half, 256 * (half + 1))
             layer2_half(last, half)
             tanh_half(last, half)
+        for half in range(2):
+            store("v", last - 1, half)
         for half in range(2):
             turn_out(last, half)
             store("v", last, half)

@@ -22,9 +22,6 @@ FLOPS = 2 * E * (D + 1) * MID + 2 * E * MID * OUT
 TOK = 512
 TILES = E // TOK
 SUBS = TOK // P
-RELU_S = 0
-RELU_S0 = 0
-GC = "gg"
 
 
 def tile_edgenetwork_t_kernel(tc, dst_feat, dst_hidden, src_feat, src_bytes, src_scale,
@@ -67,20 +64,23 @@ def tile_edgenetwork_t_kernel(tc, dst_feat, dst_hidden, src_feat, src_bytes, src
             nc.sync.dma_start(out=w1_rows[h][:],
                               in_=w1[512 * h:512 * (h + 1), 0:D].rearrange("(p t) k -> p t k", t=4))
 
-        with nc.allow_non_contiguous_dma(reason="one bfloat16 of each row of W1"):
-            for h in range(2):
-                nc.scalar.dma_start(out=w_bf[h][:, :, 0:1],
-                                    in_=w1[512 * h:512 * (h + 1), D:D + 1].rearrange("(p t) o -> p t o", t=4))
-                if h == 0:
-                    nc.scalar.dma_start(out=b1_bf[:], in_=b1.rearrange("(h p t) -> p h t", h=2, t=4))
         nc.scalar.activation(out=warm[:], in_=warm[:], func=ACT.Tanh)
-        load_edge(0)
+
+        def load_w_col(h):
+            with nc.allow_non_contiguous_dma(reason="one bfloat16 of each row of W1"):
+                nc.sync.dma_start(out=w_bf[h][:, :, 0:1],
+                                  in_=w1[512 * h:512 * (h + 1), D:D + 1].rearrange("(p t) o -> p t o", t=4))
+
+        load_w1(0)
         nc.sync.dma_start(out=scale_bc[:], in_=src_scale.rearrange("o k -> (o k)").partition_broadcast(P))
         load_x(0, 0, 2)
-        load_w1(0)
+        load_w_col(0)
+        nc.sync.dma_start(out=b1_bf[:], in_=b1.rearrange("(h p t) -> p h t", h=2, t=4))
+        load_edge(0)
         load_x(0, 2, SUBS)
-        load_edge(1)
+        load_w_col(1)
         load_w1(1)
+        load_edge(1)
         load_x(1)
         nc.sync.dma_start(out=w2_rows[:], in_=w2.rearrange("(p c) k -> p c k", c=2))
         nc.sync.dma_start(out=b2_bf[:], in_=b2.rearrange("(p c) -> p c", c=2))
@@ -183,9 +183,9 @@ def tile_edgenetwork_t_kernel(tc, dst_feat, dst_hidden, src_feat, src_bytes, src
                 ht = work.tile([P, TOK, 4], BF16, name="hidden", bufs=4, align_bytes=64)
                 hb[i, h] = ht
             cols = slice(P * s, P * (s + 1))
-            nc.vector.tensor_tensor(out=hb[i, h][:, cols, :].rearrange("p (c i) t -> p c t i", i=4),
-                                    in0=mm.pop((i, h, s))[:].rearrange("p t (c i) -> p c t i", i=4),
-                                    in1=cs[i][:, 4 * h:4 * (h + 1), cols].rearrange("p t (c i) -> p c t i", i=4),
+            nc.vector.tensor_tensor(out=hb[i, h][:, cols, :].rearrange("p (c i) t -> p c t i", i=2),
+                                    in0=mm.pop((i, h, s))[:].rearrange("p t (c i) -> p c t i", i=2),
+                                    in1=cs[i][:, 4 * h:4 * (h + 1), cols].rearrange("p t (c i) -> p c t i", i=2),
                                     op=ADD)
 
         def relu(eng, i, h, lo, hi):
@@ -268,27 +268,25 @@ def tile_edgenetwork_t_kernel(tc, dst_feat, dst_hidden, src_feat, src_bytes, src
             banks["w2", h] = bank
             turn(bank, [w2_rows[:, c, 512 * h:512 * (h + 1)].bitcast(F32) for c in range(2)])
 
-        nc.vector.tensor_copy(out=w_col[:, 0, :], in_=w_bf[0][:, :, 0])
-        nc.vector.tensor_copy(out=b1_col[:], in_=b1_bf[:])
-        nc.vector.tensor_copy(out=w_col[:, 1, :], in_=w_bf[1][:, :, 0])
-        nc.gpsimd.tensor_copy(out=b2_col[:], in_=b2_bf[:])
-
-        for t in range(3):
-            make_c("s", 0, t)
+        turn_w1(0, 0)
+        turn_w1(0, 1)
+        unbank("s", w1_words[0], 0, banks.pop(("w", 0, 0)))
+        unbank("v", w1_words[0], 1, banks.pop(("w", 0, 1)))
         widen(0, 0)
         widen(0, 1)
-        for t in range(3, 8):
-            make_c("v", 0, t)
+        quantize(w1_codes[0], w1_scales[0], w1_words[0])
+        nc.vector.tensor_copy(out=w_col[:, 0, :], in_=w_bf[0][:, :, 0])
+        nc.vector.tensor_copy(out=b1_col[:], in_=b1_bf[:])
         turn_x(0, 0)
         copy_x("s", 0, 0)
-        turn_w1(0, 0)
+        make_c("s", 0, 0)
+        make_c("v", 0, 2)
         quant_x(0, 0, 256)
-        unbank("s", w1_words[0], 0, banks.pop(("w", 0, 0)))
-        turn_w1(0, 1)
-        unbank("v", w1_words[0], 1, banks.pop(("w", 0, 1)))
-        quantize(w1_codes[0], w1_scales[0], w1_words[0])
+        make_c("s", 0, 1)
+        make_c("v", 0, 3)
         widen(0, 2)
         widen(0, 3)
+
         last = TILES - 1
         steps = [(i, g) for i in range(TILES) for g in range(4)]
 
@@ -303,20 +301,23 @@ def tile_edgenetwork_t_kernel(tc, dst_feat, dst_hidden, src_feat, src_bytes, src
         layer1_step(0, 0)
         turn_x(0, 1)
         copy_x("s", 0, 1)
-        turn_w1(1, 0)
-        unbank("s", w1_words[1], 0, banks.pop(("w", 1, 0)))
-        make_c("s", 1, 0)
         add_step(0, 0)
+        nc.vector.tensor_copy(out=w_col[:, 1, :], in_=w_bf[1][:, :, 0])
+        for t in range(4, 8):
+            make_c("gs"[t % 2], 0, t)
         quant_x(0, 256, TOK)
+        turn_w1(1, 0)
         layer1_step(0, 1)
         turn_w1(1, 1)
+        unbank("s", w1_words[1], 0, banks.pop(("w", 1, 0)))
         unbank("s", w1_words[1], 1, banks.pop(("w", 1, 1)))
-        for t in range(1, 4):
-            make_c("s", 1, t)
+        for t in range(4):
+            make_c("gs"[t % 2], 1, t)
         for s in range(SUBS):
             widen(1, s)
         add_step(0, 1)
         quantize(w1_codes[1], w1_scales[1], w1_words[1])
+        relu("v", 0, 0, 0, TOK)
         layer1_step(0, 2)
         for n, (i, g) in enumerate(steps):
             nxt = i < last
@@ -324,10 +325,11 @@ def tile_edgenetwork_t_kernel(tc, dst_feat, dst_hidden, src_feat, src_bytes, src
             if n > 1:
                 if n + 1 < len(steps):
                     layer1_step(*steps[n + 1])
-                add_step(i, g)
+                if n + 1 < len(steps):
+                    add_step(i, g)
             if g == 0:
                 if prev:
-                    relu("v", i - 1, 1, RELU_S, TOK)
+                    relu("v", i - 1, 1, 0, TOK)
                 if prev and nxt:
                     copy_x("s", i + 1, 1)
                     copy_x("s", i + 1, 0)
@@ -342,30 +344,31 @@ def tile_edgenetwork_t_kernel(tc, dst_feat, dst_hidden, src_feat, src_bytes, src
                     turn_out(i - 2, 0)
                     turn_out(i - 2, 1)
                 if i == 1:
+                    nc.gpsimd.tensor_copy(out=b2_col[:], in_=b2_bf[:])
                     turn_w2(0)
                     turn_w2(1)
-                if RELU_S0:
-                    relu("s", i, 0, 0, RELU_S0)
                 if prev:
                     quant_h(i - 1, 1)
                     if nxt:
                         quant_x(i + 1)
                 else:
-                    for s in range(SUBS):
-                        widen(2, s)
                     copy_x("s", 1, 1)
                     copy_x("s", 1, 0)
                 if i > 1:
                     store("s", i - 2, 1)
                     store("s", i - 2, 0)
                 if nxt:
-                    make_c(GC[0], i + 1, 6)
-                    make_c(GC[1], i + 1, 7)
+                    make_c("g", i + 1, 6)
+                    make_c("g", i + 1, 7)
                 if i == 1:
                     unbank("s", w2_words, 1, banks.pop(("w2", 1)))
                     unbank("s", w2_words, 0, banks.pop(("w2", 0)))
             if g == 2:
-                relu("v", i, 0, RELU_S0, TOK)
+                if prev:
+                    relu("v", i, 0, 0, TOK)
+                if i == 0:
+                    for s in range(SUBS):
+                        widen(2, s)
                 if i + 3 < TILES:
                     widen_off_vector(i + 3)
                 if i == 1:
@@ -377,30 +380,41 @@ def tile_edgenetwork_t_kernel(tc, dst_feat, dst_hidden, src_feat, src_bytes, src
                 if i + 2 < TILES:
                     make_c("s", i + 2, 0)
                     make_c("s", i + 2, 1)
-            if g == 3:
+            if g == 3 and nxt:
                 quant_h(i, 0)
+            if g == 3:
                 if prev:
                     tanh(i - 1, 1)
                     tanh(i - 1, 0)
                 if i + 2 < TILES:
                     turn_x(i + 2, 0)
                     turn_x(i + 2, 1)
-                if nxt and RELU_S:
-                    relu("s", i, 1, 0, RELU_S)
                 if i + 2 < TILES:
                     make_c("s", i + 2, 2)
                     make_c("s", i + 2, 3)
 
+        turn_out(last - 1, 0)
+        turn_out(last - 1, 1)
+        store("s", last - 1, 1)
+        store("s", last - 1, 0)
+        add(last, 1, 3)
         relu("v", last, 1, 0, 256)
-        relu("s", last, 1, 256, TOK)
-        for half in range(2):
-            turn_out(last - 1, half)
-        for half in range(2):
-            quant_h(last, 1, 256 * half, 256 * (half + 1))
-            layer2_half(last, half)
-            tanh_half(last, half)
-        for half in range(2):
-            store("v", last - 1, half)
-        for half in range(2):
-            turn_out(last, half)
-            store("v", last, half)
+        quant_h(last, 0)
+        quant_h(last, 1, 0, 256)
+        add(last, 1, 2)
+        relu("v", last, 1, 256, TOK)
+        quant_h(last, 1, 256, TOK)
+        layer2_half(last, 0)
+        tanh_half(last, 0)
+        layer2_half(last, 1)
+        tanh_half(last, 1)
+        turn_out(last, 0)
+        store("v", last, 0)
+        for s, eng in ((2, "s"), (3, "v")):
+            bank = psum.tile([P, 2, P], F32, name="acc", bufs=4)
+            for c in range(2):
+                nc.tensor.transpose(bank[:, c, :], ob[last][:, c, P * s:P * (s + 1)], ident[:])
+            res = work.tile([P, OUT], F32, name="last_result")
+            copy(eng, res[:].rearrange("p (q c) -> p q c", c=2), bank[:].rearrange("p c q -> p q c"))
+            r0 = TOK * last + P * s
+            nc.sync.dma_start(out=out[r0:r0 + P, :], in_=res[:])

from contextlib import ExitStack

import concourse.mybir as mybir
from concourse.masks import make_identity

F32 = mybir.dt.float32
BF16 = mybir.dt.bfloat16
U32 = mybir.dt.uint32
U8 = mybir.dt.uint8
FP8 = mybir.dt.float8_e4m3fn
FP8X4 = mybir.dt.float8_e4m3fn_x4
ADD = mybir.AluOpType.add
MULT = mybir.AluOpType.mult
MAX = mybir.AluOpType.max
ACT = mybir.ActivationFunctionType

P = 128
E, F, H, MID, OUT = 4096, 64, 192, 1024, 256
D = 2 * (F + H)
FLOPS = 2 * E * (D + 1) * MID + 2 * E * MID * OUT

TOK = 512
TILES = E // TOK
SUBS = TOK // P


def tile_edgenetwork_t_kernel(tc, dst_feat, dst_hidden, src_feat, src_bytes, src_scale,
                                          edge, w1, b1, w2, b2, out):
    nc = tc.nc
    with ExitStack() as ctx:
        keep = ctx.enter_context(tc.tile_pool(name="keep", bufs=1))
        work = ctx.enter_context(tc.tile_pool(name="work", bufs=2))
        psum = ctx.enter_context(tc.psum_pool(name="psum", bufs=2))
        ctx.enter_context(tc.manual_schedule())

        ident = keep.tile([P, P], F32, name="ident")
        make_identity(nc, ident[:])
        warm = keep.tile([P, 1], F32, name="warm")
        nc.vector.memset(warm[:], 0.0)

        scale_bc = keep.tile([P, H], F32, name="scale_bc")
        edge_bc = [keep.tile([P, TOK], BF16, name=f"edge_bc{i}") for i in range(TILES)]
        x_rows = [keep.tile([P, SUBS, D], BF16, name=f"x_rows{i}", align_bytes=64) for i in range(TILES)]
        x_bytes = [keep.tile([P, SUBS, H], U8, name=f"x_bytes{i}", align_bytes=64) for i in range(TILES)]
        w1_rows = [keep.tile([P, 4, D], BF16, name=f"w1_rows{h}", align_bytes=64) for h in range(2)]
        w2_rows = keep.tile([P, 2, MID], BF16, name="w2_rows", align_bytes=64)
        w_bf = [keep.tile([P, 4, 2], BF16, name=f"w_bf{h}") for h in range(2)]
        b1_bf = keep.tile([P, 2, 4], BF16, name="b1_bf")
        b2_bf = keep.tile([P, 2], BF16, name="b2_bf")

        def load_x(i, s0=0, s1=SUBS):
            def rows(ap):
                return ap[TOK * i + P * s0:TOK * i + P * s1, :].rearrange("(s p) f -> p s f", p=P)

            nc.sync.dma_start(out=x_bytes[i][:, s0:s1, :], in_=rows(src_bytes))
            nc.sync.dma_start(out=x_rows[i][:, s0:s1, 0:F], in_=rows(dst_feat))
            nc.sync.dma_start(out=x_rows[i][:, s0:s1, F:F + H], in_=rows(dst_hidden))
            nc.sync.dma_start(out=x_rows[i][:, s0:s1, F + H:2 * F + H], in_=rows(src_feat))

        def load_edge(i):
            nc.sync.dma_start(out=edge_bc[i][:], in_=edge[TOK * i:TOK * (i + 1)].partition_broadcast(P))

        def load_w1(h):
            nc.sync.dma_start(out=w1_rows[h][:],
                              in_=w1[512 * h:512 * (h + 1), 0:D].rearrange("(p t) k -> p t k", t=4))

        nc.scalar.activation(out=warm[:], in_=warm[:], func=ACT.Tanh)

        def load_w_col(h):
            with nc.allow_non_contiguous_dma(reason="one bfloat16 of each row of W1"):
                nc.sync.dma_start(out=w_bf[h][:, :, 0:1],
                                  in_=w1[512 * h:512 * (h + 1), D:D + 1].rearrange("(p t) o -> p t o", t=4))

        load_w1(0)
        nc.sync.dma_start(out=scale_bc[:], in_=src_scale.rearrange("o k -> (o k)").partition_broadcast(P))
        load_x(0, 0, 2)
        load_w_col(0)
        nc.sync.dma_start(out=b1_bf[:], in_=b1.rearrange("(h p t) -> p h t", h=2, t=4))
        load_edge(0)
        load_x(0, 2, SUBS)
        load_w_col(1)
        load_w1(1)
        load_edge(1)
        load_x(1)
        nc.sync.dma_start(out=w2_rows[:], in_=w2.rearrange("(p c) k -> p c k", c=2))
        nc.sync.dma_start(out=b2_bf[:], in_=b2.rearrange("(p c) -> p c", c=2))
        for i in range(2, TILES):
            load_x(i)
            load_edge(i)

        w_col = keep.tile([P, 2, 4], F32, name="w_col")
        b1_col = keep.tile([P, 2, 4], F32, name="b1_col")
        b2_col = keep.tile([P, 2], F32, name="b2_col")
        w1_words = [keep.tile([P, 512, 2], F32, name=f"w1_words{h}", align_bytes=64) for h in range(2)]
        w2_words = keep.tile([P, 512, 2], F32, name="w2_words", align_bytes=64)
        w1_codes = [keep.tile([P, 512], U32, name=f"w1_codes{h}", align_bytes=64) for h in range(2)]
        w1_scales = [keep.tile([P, 512], U8, name=f"w1_scales{h}", align_bytes=64) for h in range(2)]
        w2_codes = keep.tile([P, 512], U32, name="w2_codes", align_bytes=64)
        w2_scales = keep.tile([P, 512], U8, name="w2_scales", align_bytes=64)

        def quantize(codes, scales, words, lo=0, hi=512):
            nc.vector.quantize_mx(out=codes[:, lo:hi].bitcast(FP8X4), scales=scales[:, lo:hi],
                                  in_=words[:, lo:hi, :].rearrange("p n u -> p (n u)").bitcast(BF16))

        def bank4():
            return psum.tile([P, 2, 2, P], F32, name="turned", bufs=2)

        def turn(bank, pairs):
            for a, words in enumerate(pairs):
                for u in range(2):
                    nc.tensor.transpose(bank[:, a, u, :], words[:, u:256:2], ident[:])

        def copy(eng, out_ap, in_ap):
            if eng == "s":
                nc.scalar.copy(out=out_ap, in_=in_ap)
            else:
                nc.vector.tensor_copy(out=out_ap, in_=in_ap)

        def unbank(eng, words, half, bank):
            copy(eng, words[:, 256 * half:256 * (half + 1), :].rearrange("p (a n) u -> p a n u", a=2),
                 bank[:].rearrange("p a u n -> p a n u"))

        xw, xc, xs, banks = {}, {}, {}, {}

        def widen(i, s):
            nc.vector.tensor_tensor(out=x_rows[i][:, s, 2 * F + H:D], in0=x_bytes[i][:, s, :].bitcast(FP8),
                                    in1=scale_bc[:], op=MULT)

        def widen_off_vector(i):
            wide = work.tile([P, SUBS, H], BF16, name="wide")
            nc.scalar.copy(out=wide[:].rearrange("p s f -> p (s f)"),
                           in_=x_bytes[i][:].rearrange("p s f -> p (s f)").bitcast(FP8))
            for s in range(SUBS):
                nc.gpsimd.tensor_tensor(out=x_rows[i][:, s, 2 * F + H:D], in0=wide[:, s, :], in1=scale_bc[:], op=MULT)

        def turn_x(i, half):
            bank = bank4()
            banks[i, half] = bank
            turn(bank, [x_rows[i][:, 2 * half + a, :].bitcast(F32) for a in range(2)])

        def copy_x(eng, i, half):
            if i not in xw:
                xt = work.tile([P, TOK, 2], F32, name="x_words", align_bytes=64)
                xw[i] = xt
            unbank(eng, xw[i], half, banks.pop((i, half)))

        def quant_x(i, lo=0, hi=TOK):
            if lo == 0:
                codes = work.tile([P, TOK], U32, name="x_codes", bufs=3, align_bytes=64)
                scales = work.tile([P, TOK], U8, name="x_scales", bufs=3, align_bytes=64)
                xc[i], xs[i] = codes, scales
            quantize(xc[i], xs[i], xw[i], lo, hi)

        cs = {}

        def make_c(eng, i, ht):
            if i not in cs:
                ct = work.tile([P, 8, TOK], F32, name="edge_term", bufs=3)
                cs[i] = ct
            h, t = ht // 4, ht % 4
            o, w_ap, b_ap = cs[i][:, ht, :], w_col[:, h, t:t + 1], b1_col[:, h, t:t + 1]
            if eng == "s":
                nc.scalar.activation(out=o, in_=edge_bc[i][:], func=ACT.Identity, scale=w_ap, bias=b_ap)
            elif eng == "v":
                nc.vector.tensor_scalar(out=o, in0=edge_bc[i][:], scalar1=w_ap, scalar2=b_ap, op0=MULT, op1=ADD)
            else:
                nc.gpsimd.tensor_scalar(out=o, in0=edge_bc[i][:], scalar1=w_ap, scalar2=b_ap, op0=MULT, op1=ADD)

        mm, hb, hc, hs = {}, {}, {}, {}

        def layer1(i, h, s):
            acc = psum.tile([P, 4, P], F32, name="acc", bufs=4)
            for t in range(4):
                nc.tensor.matmul_mx(out=acc[:, t, :],
                                    lhsT=w1_codes[h][:, P * t:P * (t + 1)].bitcast(FP8X4),
                                    lhsT_scale=w1_scales[h][:, P * t:P * (t + 1)],
                                    rhs=xc[i][:, P * s:P * (s + 1)].bitcast(FP8X4),
                                    rhs_scale=xs[i][:, P * s:P * (s + 1)], start=True, stop=True)
            mm[i, h, s] = acc

        def add(i, h, s):
            if (i, h) not in hb:
                ht = work.tile([P, TOK, 4], BF16, name="hidden", bufs=4, align_bytes=64)
                hb[i, h] = ht
            cols = slice(P * s, P * (s + 1))
            nc.vector.tensor_tensor(out=hb[i, h][:, cols, :].rearrange("p (c i) t -> p c t i", i=2),
                                    in0=mm.pop((i, h, s))[:].rearrange("p t (c i) -> p c t i", i=2),
                                    in1=cs[i][:, 4 * h:4 * (h + 1), cols].rearrange("p t (c i) -> p c t i", i=2),
                                    op=ADD)

        def relu(eng, i, h, lo, hi):
            part = hb[i, h][:, lo:hi, :].rearrange("p n t -> p (n t)")
            if eng == "s":
                nc.scalar.activation(out=part, in_=part, func=ACT.Relu)
            else:
                nc.vector.tensor_scalar_max(out=part, in0=part, scalar1=0.0)

        def quant_h(i, h, lo=0, hi=TOK):
            if lo == 0:
                codes = work.tile([P, TOK], U32, name="h_codes", bufs=4, align_bytes=64)
                scales = work.tile([P, TOK], U8, name="h_scales", bufs=4, align_bytes=64)
                hc[i, h], hs[i, h] = codes, scales
            nc.vector.quantize_mx(out=hc[i, h][:, lo:hi].bitcast(FP8X4), scales=hs[i, h][:, lo:hi],
                                  in_=hb[i, h][:, lo:hi, :].rearrange("p n t -> p (n t)"))

        l2, ob = {}, {}

        def layer2(i):
            for c in range(2):
                acc2 = psum.tile([P, TOK], F32, name="acc2", bufs=2)
                for h in range(2):
                    w0 = 256 * h + P * c
                    nc.tensor.matmul_mx(out=acc2[:],
                                        lhsT=w2_codes[:, w0:w0 + P].bitcast(FP8X4), lhsT_scale=w2_scales[:, w0:w0 + P],
                                        rhs=hc[i, h][:].bitcast(FP8X4), rhs_scale=hs[i, h][:],
                                        start=(h == 0), stop=(h == 1))
                l2[i, c] = acc2

        def layer2_half(i, half):
            n0 = 256 * half
            acc2 = psum.tile([P, 2, 256], F32, name="acc2", bufs=2)
            for c in range(2):
                for h in range(2):
                    w0 = 256 * h + P * c
                    nc.tensor.matmul_mx(out=acc2[:, c, :],
                                        lhsT=w2_codes[:, w0:w0 + P].bitcast(FP8X4), lhsT_scale=w2_scales[:, w0:w0 + P],
                                        rhs=hc[i, h][:, n0:n0 + 256].bitcast(FP8X4), rhs_scale=hs[i, h][:, n0:n0 + 256],
                                        start=(h == 0), stop=(h == 1))
            if i not in ob:
                ot = work.tile([P, 2, TOK], F32, name="channels", bufs=3)
                ob[i] = ot
            l2[i, half] = acc2

        def tanh_half(i, half):
            acc2 = l2.pop((i, half))
            for c in range(2):
                nc.scalar.activation(out=ob[i][:, c, 256 * half:256 * (half + 1)], in_=acc2[:, c, :],
                                     func=ACT.Tanh, bias=b2_col[:, c:c + 1])

        def tanh(i, c):
            if i not in ob:
                ot = work.tile([P, 2, TOK], F32, name="channels", bufs=3)
                ob[i] = ot
            nc.scalar.activation(out=ob[i][:, c, :], in_=l2.pop((i, c))[:], func=ACT.Tanh, bias=b2_col[:, c:c + 1])

        def turn_out(i, half):
            bank = bank4()
            banks["o", i, half] = bank
            for a in range(2):
                s = 2 * half + a
                for c in range(2):
                    nc.tensor.transpose(bank[:, a, c, :], ob[i][:, c, P * s:P * (s + 1)], ident[:])

        def store(eng, i, half):
            res = work.tile([P, 2, OUT], F32, name="result", bufs=4)
            copy(eng, res[:].rearrange("p a (q c) -> p a q c", c=2),
                 banks.pop(("o", i, half))[:].rearrange("p a c q -> p a q c"))
            r0 = TOK * i + 2 * P * half
            nc.sync.dma_start(out=out[r0:r0 + 2 * P, :].rearrange("(a p) f -> p a f", p=P), in_=res[:])

        def turn_w1(h, half):
            bank = bank4()
            banks["w", h, half] = bank
            turn(bank, [w1_rows[h][:, 2 * half + a, 0:D].bitcast(F32) for a in range(2)])

        def turn_w2(h):
            bank = bank4()
            banks["w2", h] = bank
            turn(bank, [w2_rows[:, c, 512 * h:512 * (h + 1)].bitcast(F32) for c in range(2)])

        turn_w1(0, 0)
        turn_w1(0, 1)
        unbank("s", w1_words[0], 0, banks.pop(("w", 0, 0)))
        unbank("v", w1_words[0], 1, banks.pop(("w", 0, 1)))
        widen(0, 0)
        widen(0, 1)
        quantize(w1_codes[0], w1_scales[0], w1_words[0])
        nc.vector.tensor_copy(out=w_col[:, 0, :], in_=w_bf[0][:, :, 0])
        nc.vector.tensor_copy(out=b1_col[:], in_=b1_bf[:])
        turn_x(0, 0)
        copy_x("s", 0, 0)
        make_c("s", 0, 0)
        make_c("v", 0, 2)
        quant_x(0, 0, 256)
        make_c("s", 0, 1)
        make_c("v", 0, 3)
        widen(0, 2)
        widen(0, 3)

        last = TILES - 1
        steps = [(i, g) for i in range(TILES) for g in range(4)]

        def layer1_step(i, g):
            for s in (2 * (g % 2), 2 * (g % 2) + 1):
                layer1(i, g // 2, s)

        def add_step(i, g):
            for s in (2 * (g % 2) + 1, 2 * (g % 2)):
                add(i, g // 2, s)

        layer1_step(0, 0)
        turn_x(0, 1)
        copy_x("s", 0, 1)
        add_step(0, 0)
        nc.vector.tensor_copy(out=w_col[:, 1, :], in_=w_bf[1][:, :, 0])
        for t in range(4, 8):
            make_c("gs"[t % 2], 0, t)
        quant_x(0, 256, TOK)
        turn_w1(1, 0)
        layer1_step(0, 1)
        turn_w1(1, 1)
        unbank("s", w1_words[1], 0, banks.pop(("w", 1, 0)))
        unbank("s", w1_words[1], 1, banks.pop(("w", 1, 1)))
        for t in range(4):
            make_c("gs"[t % 2], 1, t)
        for s in range(SUBS):
            widen(1, s)
        add_step(0, 1)
        quantize(w1_codes[1], w1_scales[1], w1_words[1])
        relu("v", 0, 0, 0, TOK)
        layer1_step(0, 2)
        for n, (i, g) in enumerate(steps):
            nxt = i < last
            prev = i > 0
            if n > 1:
                if n + 1 < len(steps):
                    layer1_step(*steps[n + 1])
                if n + 1 < len(steps):
                    add_step(i, g)
            if g == 0:
                if prev:
                    relu("v", i - 1, 1, 0, TOK)
                if prev and nxt:
                    copy_x("s", i + 1, 1)
                    copy_x("s", i + 1, 0)
                if i == 0:
                    turn_x(1, 0)
                    turn_x(1, 1)
                if nxt:
                    make_c("s", i + 1, 4)
                    make_c("s", i + 1, 5)
            if g == 1:
                if i > 1:
                    turn_out(i - 2, 0)
                    turn_out(i - 2, 1)
                if i == 1:
                    nc.gpsimd.tensor_copy(out=b2_col[:], in_=b2_bf[:])
                    turn_w2(0)
                    turn_w2(1)
                if prev:
                    quant_h(i - 1, 1)
                    if nxt:
                        quant_x(i + 1)
                else:
                    copy_x("s", 1, 1)
                    copy_x("s", 1, 0)
                if i > 1:
                    store("s", i - 2, 1)
                    store("s", i - 2, 0)
                if nxt:
                    make_c("g", i + 1, 6)
                    make_c("g", i + 1, 7)
                if i == 1:
                    unbank("s", w2_words, 1, banks.pop(("w2", 1)))
                    unbank("s", w2_words, 0, banks.pop(("w2", 0)))
            if g == 2:
                if prev:
                    relu("v", i, 0, 0, TOK)
                if i == 0:
                    for s in range(SUBS):
                        widen(2, s)
                if i + 3 < TILES:
                    widen_off_vector(i + 3)
                if i == 1:
                    quantize(w2_codes, w2_scales, w2_words)
                if prev:
                    layer2(i - 1)
                if i == 0:
                    quant_x(1)
                if i + 2 < TILES:
                    make_c("s", i + 2, 0)
                    make_c("s", i + 2, 1)
            if g == 3 and nxt:
                quant_h(i, 0)
            if g == 3:
                if prev:
                    tanh(i - 1, 1)
                    tanh(i - 1, 0)
                if i + 2 < TILES:
                    turn_x(i + 2, 0)
                    turn_x(i + 2, 1)
                if i + 2 < TILES:
                    make_c("s", i + 2, 2)
                    make_c("s", i + 2, 3)

        turn_out(last - 1, 0)
        turn_out(last - 1, 1)
        store("s", last - 1, 1)
        store("s", last - 1, 0)
        add(last, 1, 3)
        relu("v", last, 1, 0, 256)
        quant_h(last, 0)
        quant_h(last, 1, 0, 256)
        add(last, 1, 2)
        relu("v", last, 1, 256, TOK)
        quant_h(last, 1, 256, TOK)
        layer2_half(last, 0)
        tanh_half(last, 0)
        layer2_half(last, 1)
        tanh_half(last, 1)
        turn_out(last, 0)
        store("v", last, 0)
        for s, eng in ((2, "s"), (3, "v")):
            bank = psum.tile([P, 2, P], F32, name="acc", bufs=4)
            for c in range(2):
                nc.tensor.transpose(bank[:, c, :], ob[last][:, c, P * s:P * (s + 1)], ident[:])
            res = work.tile([P, OUT], F32, name="last_result")
            copy(eng, res[:].rearrange("p (q c) -> p q c", c=2), bank[:].rearrange("p c q -> p q c"))
            r0 = TOK * last + P * s
            nc.sync.dma_start(out=out[r0:r0 + P, :], in_=res[:])
